import numpy as np
import ml_dtypes


def mxq(x, axis, fmt="e4m3"):
    dtype, down = {"e4m3": (ml_dtypes.float8_e4m3fn, 7), "e5m2": (ml_dtypes.float8_e5m2, 14)}[fmt]
    v = np.moveaxis(np.asarray(x, np.float32).astype(ml_dtypes.bfloat16).astype(np.float64), axis, -1)
    blocks = v.reshape(v.shape[:-1] + (-1, 32))
    amax = np.abs(blocks).max(-1, keepdims=True)
    byte = np.maximum(np.where(amax > 0, np.frexp(amax)[1] - 1 + 127, 0) - down, 1)
    scale = np.exp2(byte - 127.0)
    codes = (blocks / scale).astype(np.float32).astype(dtype).astype(np.float64)
    return np.moveaxis((codes * scale).reshape(v.shape), -1, axis)


WIDE = False


def mx_kscale(k):
    if not WIDE:
        return np.ones(k)
    levels = np.array([10, -10, 5, -5, 0])
    if k % 512:
        return np.exp2(np.random.permutation(np.resize(levels, k // 32))).repeat(32)
    a = np.empty((k // 512, 16))
    for p in range(k // 512):
        a[p, :8] = np.random.permutation(np.resize(levels, 8))
        for g in range(8):
            far = levels[np.abs(levels - a[p, g]) >= 10]
            a[p, g + 8] = far[np.random.randint(len(far))]
    return np.exp2(a.ravel()).repeat(32)


BF16 = ml_dtypes.bfloat16


def bf(x):
    return np.asarray(x, np.float32).astype(BF16)


def f64(x):
    return np.asarray(x).astype(np.float64)


B, S, D, R, C = 128, 32, 512, 16, 1024
MIN_SCALE = 1e-3
TEMPERATURE = 1.5


def softplus(v):
    return np.logaddexp(v, 0.0)


def setup_inputs():
    s = mx_kscale(D)
    return {
        "features": bf(np.random.standard_normal((B, D)) * 0.3 * s),
        "W_diag": bf(np.random.standard_normal((D, D)) * 2.0 / np.sqrt(D) / s[None, :]),
        "b_diag": bf(-4.0 + 0.2 * np.random.standard_normal(D)),
        "W_cls": bf(np.random.standard_normal((C, D)) * 3.0 / np.sqrt(D) / s[None, :]),
        "b_cls": bf(np.random.standard_normal(C) * 0.3),
        "noise_diag": bf(np.random.standard_normal((B, S, D)) * 10.0 * s),
        "lr_samples": bf(np.random.standard_normal((B, S, D)) * 0.3 * s),
    }


def reference(features, W_diag, b_diag, W_cls, b_cls, noise_diag, lr_samples):
    f = f64(features)
    z = (mxq(f, 1, "e4m3") @ mxq(f64(W_diag), 1, "e4m3").T) + f64(b_diag)
    diagonal_std = softplus(z) + MIN_SCALE
    samples = f64(lr_samples) + diagonal_std[:, None, :] * f64(noise_diag)
    pre_logits = f[:, None, :] + samples
    logits = (mxq(pre_logits, 2, "e4m3") @ mxq(f64(W_cls), 1, "e4m3").T) + f64(b_cls)
    return logits / TEMPERATURE

@@ -1,0 +1,291 @@
+from contextlib import ExitStack
+
+import concourse.mybir as mybir
+from concourse.masks import make_identity
+
+F32 = mybir.dt.float32
+BF16 = mybir.dt.bfloat16
+U32 = mybir.dt.uint32
+U8 = mybir.dt.uint8
+FP8X4 = mybir.dt.float8_e4m3fn_x4
+ACT = mybir.ActivationFunctionType
+ALU = mybir.AluOpType
+
+P = 128
+PAIR = 2
+HALVES = 2
+PACK = HALVES * PAIR
+B, S, D, C = 128, 32, 512, 1024
+assert D == P * PACK
+
+ROW_TILES = 2
+BLOCK_ROWS = ROW_TILES * P
+BLOCKS = B * S // BLOCK_ROWS
+BLOCKS_PER_LOAD = 4
+LOADS = BLOCKS // BLOCKS_PER_LOAD
+EXAMPLES = BLOCK_ROWS // S
+EXAMPLE_COLS = P // EXAMPLES
+N_COLS = 512
+SHIFT_AHEAD = 2
+ADD_AHEAD = 1
+BANKS = ROW_TILES * (C // N_COLS)
+SCALAR_BANKS = 1
+MIN_SCALE = 1e-3
+INV_TEMPERATURE = 1.0 / 1.5
+
+FLOPS = 2 * B * S * D * C + 2 * B * D * D
+
+
+def turn_row_tiles(nc, bank, rows, identity):
+    for i in range(rows.shape[1]):
+        words = rows[:, i, :].bitcast(F32)
+        for u in range(HALVES):
+            nc.tensor.transpose(bank[:, i, u, :], words[:, u : HALVES * P : HALVES], identity)
+
+
+def halves_together(bank):
+    return bank.rearrange("p i u r -> p i r u")
+
+
+def quantise(nc, codes, scales, grouped):
+    nc.vector.quantize_mx(
+        out=codes.bitcast(FP8X4),
+        scales=scales,
+        in_=grouped.rearrange("p i r t -> p (i r t)"),
+    )
+
+
+def tile_hetxlhead_pa_kernel(
+    tc, features, W_diag, b_diag, W_cls, b_cls, noise_diag, lr_samples, out
+):
+    nc = tc.nc
+    noise_loads = noise_diag.rearrange("b s d -> (b s) d").rearrange(
+        "(l j p i) d -> l p j i d", j=BLOCKS_PER_LOAD, p=P, i=ROW_TILES
+    )
+    lr_loads = lr_samples.rearrange("b s d -> (b s) d").rearrange(
+        "(l j p i) d -> l p j i d", j=BLOCKS_PER_LOAD, p=P, i=ROW_TILES
+    )
+    out_blocks = out.rearrange("b s c -> (b s) c").rearrange(
+        "(j p i) c -> j p i c", p=P, i=ROW_TILES
+    )
+
+    with ExitStack() as ctx:
+        keep = ctx.enter_context(tc.tile_pool(name="keep", bufs=1))
+        work = ctx.enter_context(tc.tile_pool(name="work", bufs=3))
+        results = ctx.enter_context(tc.tile_pool(name="results", bufs=3))
+        turned = ctx.enter_context(tc.psum_pool(name="turned", bufs=4))
+        sums = ctx.enter_context(tc.psum_pool(name="sums", bufs=4))
+
+        def turn_weight(grouped, rows):
+            for g in range(rows.shape[1] // ROW_TILES):
+                pair = slice(g * ROW_TILES, (g + 1) * ROW_TILES)
+                bank = turned.tile([P, ROW_TILES, HALVES, P], F32, tag="turned")
+                turn_row_tiles(nc, bank[:], rows[:, pair], identity[:])
+                if g % 2 == 0:
+                    nc.vector.tensor_copy(
+                        out=grouped[:, pair].bitcast(F32), in_=halves_together(bank[:])
+                    )
+                else:
+                    nc.scalar.copy(out=grouped[:, pair].bitcast(F32), in_=halves_together(bank[:]))
+
+        identity = keep.tile([P, P], F32)
+        make_identity(nc, identity[:])
+        one = keep.tile([P, 1], F32)
+        nc.vector.memset(one[:], 1.0)
+        warm = keep.tile([P, 1], F32)
+        nc.scalar.activation(out=warm[:], in_=one[:], func=ACT.Exp)
+
+        feat_rows = keep.tile([P, 1, D], BF16)
+        nc.sync.dma_start(out=feat_rows[:, 0, :], in_=features)
+        wd_rows = keep.tile([P, PACK, D], BF16)
+        nc.sync.dma_start(out=wd_rows[:], in_=W_diag.rearrange("(r t) k -> r t k", t=PACK))
+        bd_rows = keep.tile([P, PACK], BF16)
+        nc.sync.dma_start(out=bd_rows[:], in_=b_diag.rearrange("(p t) -> p t", t=PACK))
+        noise_rows = []
+        lr_rows = []
+        wc_rows = keep.tile([P, C // P, D], BF16)
+        bc_rows = keep.tile([P, C], BF16)
+        for l in range(LOADS):
+            noise_rows.append(
+                keep.tile([P, BLOCKS_PER_LOAD, ROW_TILES, D], BF16, name="noise_rows%d" % l)
+            )
+            nc.sync.dma_start(out=noise_rows[l][:], in_=noise_loads[l])
+            lr_rows.append(
+                keep.tile([P, BLOCKS_PER_LOAD, ROW_TILES, D], BF16, name="lr_rows%d" % l)
+            )
+            nc.sync.dma_start(out=lr_rows[l][:], in_=lr_loads[l])
+            if l == 0:
+                nc.sync.dma_start(out=wc_rows[:], in_=W_cls.rearrange("(i r) k -> r i k", r=P))
+                nc.sync.dma_start(out=bc_rows[:], in_=b_cls.partition_broadcast(P))
+
+        head_bank = turned.tile([P, ROW_TILES, HALVES, P], F32, tag="turned")
+        turn_row_tiles(nc, head_bank[:, 0:1], feat_rows[:], identity[:])
+        feat = keep.tile([P, 1, B, PACK], BF16, align_bytes=64)
+        nc.vector.tensor_copy(out=feat[:].bitcast(F32), in_=halves_together(head_bank[:, 0:1]))
+        feat32 = keep.tile([P, HALVES, B, PAIR], F32)
+        nc.vector.tensor_copy(
+            out=feat32[:].rearrange("p u b e -> p u (b e)"), in_=head_bank[:, 0].bitcast(BF16)
+        )
+        bd = keep.tile([P, PACK], F32)
+        nc.vector.tensor_copy(out=bd[:], in_=bd_rows[:])
+
+        wd = keep.tile([P, PACK, P, PACK], BF16, align_bytes=64)
+        turn_weight(wd, wd_rows)
+        feat_codes = keep.tile([P, B], U32, align_bytes=64)
+        feat_scales = keep.tile([P, B], U8, align_bytes=64)
+        quantise(nc, feat_codes[:], feat_scales[:], feat[:])
+        wd_codes = keep.tile([P, D], U32, align_bytes=64)
+        wd_scales = keep.tile([P, D], U8, align_bytes=64)
+        quantise(nc, wd_codes[:], wd_scales[:], wd[:])
+
+        z = sums.tile([P, PACK, B], F32, tag="sums")
+        for t in range(PACK):
+            nc.tensor.matmul_mx(
+                out=z[:, t, :],
+                lhsT=wd_codes[:, t * P : (t + 1) * P].bitcast(FP8X4),
+                lhsT_scale=wd_scales[:, t * P : (t + 1) * P],
+                rhs=feat_codes[:].bitcast(FP8X4),
+                rhs_scale=feat_scales[:],
+                start=True,
+                stop=True,
+            )
+        v = keep.tile([P, PACK, B], F32)
+        nc.vector.tensor_tensor(
+            out=v[:], in0=z[:], in1=bd[:].unsqueeze(2).to_broadcast([P, PACK, B]), op=ALU.add
+        )
+        magnitude = keep.tile([P, PACK, B], F32)
+        nc.scalar.activation(out=magnitude[:], in_=v[:], func=ACT.Abs)
+        decay = keep.tile([P, PACK, B], F32)
+        nc.scalar.activation(out=decay[:], in_=magnitude[:], func=ACT.Exp, scale=-1.0)
+        log_term = keep.tile([P, PACK, B], F32)
+        nc.scalar.activation(out=log_term[:], in_=decay[:], func=ACT.Ln, bias=one[:])
+        ramp = keep.tile([P, PACK, B], F32)
+        nc.vector.tensor_scalar(
+            out=ramp[:], in0=v[:], scalar1=0.0, scalar2=MIN_SCALE, op0=ALU.max, op1=ALU.add
+        )
+        std = keep.tile([P, PACK, B], F32)
+        nc.vector.tensor_tensor(out=std[:], in0=log_term[:], in1=ramp[:], op=ALU.add)
+
+        wc = keep.tile([P, C // P, P, PACK], BF16, align_bytes=64)
+        turn_weight(wc, wc_rows)
+        wc_codes = keep.tile([P, C], U32, align_bytes=64)
+        wc_scales = keep.tile([P, C], U8, align_bytes=64)
+        quantise(nc, wc_codes[:], wc_scales[:], wc[:])
+        bias = keep.tile([P, C], F32)
+        nc.vector.tensor_scalar_mul(out=bias[:], in0=bc_rows[:], scalar1=INV_TEMPERATURE)
+
+        noise_bank, lr_bank, shifted = {}, {}, {}
+        pre, pre_codes, pre_scales, acc, result = {}, {}, {}, {}, {}
+
+        def exists(j):
+            return 0 <= j < BLOCKS
+
+        def turn(j):
+            if not exists(j):
+                return
+            l, k = divmod(j, BLOCKS_PER_LOAD)
+            noise_bank[j] = turned.tile(
+                [P, ROW_TILES, HALVES, P], F32, name="noise_bank", tag="turned"
+            )
+            turn_row_tiles(nc, noise_bank[j][:], noise_rows[l][:, k], identity[:])
+            lr_bank[j] = turned.tile([P, ROW_TILES, HALVES, P], F32, name="lr_bank", tag="turned")
+            turn_row_tiles(nc, lr_bank[j][:], lr_rows[l][:, k], identity[:])
+
+        def shift(j):
+            if not exists(j):
+                return
+            noise_turned = work.tile([P, ROW_TILES, HALVES, P, PAIR], BF16)
+            nc.scalar.copy(
+                out=noise_turned[:].rearrange("p i u r e -> p i u (r e)"),
+                in_=noise_bank[j][:].bitcast(BF16),
+            )
+            shifted[j] = work.tile([P, ROW_TILES, PACK, P], F32, name="shifted")
+            for m in range(EXAMPLES):
+                b = j * EXAMPLES + m
+                cols = slice(m * EXAMPLE_COLS, (m + 1) * EXAMPLE_COLS)
+                for t in range(PACK):
+                    u, e = divmod(t, PAIR)
+                    nc.scalar.activation(
+                        out=shifted[j][:, :, t, cols],
+                        in_=noise_turned[:, :, u, cols, e],
+                        func=ACT.Identity,
+                        scale=std[:, t, b : b + 1],
+                        bias=feat32[:, u, b, e : e + 1],
+                    )
+
+        def add_lr(j):
+            if not exists(j):
+                return
+            pre[j] = work.tile([P, ROW_TILES, P, PACK], BF16, name="pre", align_bytes=64)
+            for i in range(ROW_TILES):
+                nc.vector.tensor_tensor(
+                    out=pre[j][:, i].rearrange("p r (u e) -> p r u e", e=PAIR),
+                    in0=lr_bank[j][:, i].bitcast(BF16).rearrange("p u (r e) -> p r u e", e=PAIR),
+                    in1=shifted[j][:, i].rearrange("p (u e) r -> p r u e", e=PAIR),
+                    op=ALU.add,
+                )
+
+        def quantise_block(j):
+            if not exists(j):
+                return
+            pre_codes[j] = work.tile([P, BLOCK_ROWS], U32, name="pre_codes", align_bytes=64)
+            pre_scales[j] = work.tile([P, BLOCK_ROWS], U8, name="pre_scales", align_bytes=64)
+            quantise(nc, pre_codes[j][:], pre_scales[j][:], pre[j][:])
+
+        def multiply(j, i):
+            if not exists(j):
+                return
+            for h in range(C // N_COLS):
+                classes = slice(h * N_COLS, (h + 1) * N_COLS)
+                acc[j, i, h] = sums.tile([P, N_COLS], F32, name="acc", tag="sums")
+                nc.tensor.matmul_mx(
+                    out=acc[j, i, h][:],
+                    lhsT=pre_codes[j][:, i * P : (i + 1) * P].bitcast(FP8X4),
+                    lhsT_scale=pre_scales[j][:, i * P : (i + 1) * P],
+                    rhs=wc_codes[:, classes].bitcast(FP8X4),
+                    rhs_scale=wc_scales[:, classes],
+                    start=True,
+                    stop=True,
+                )
+
+        def finish(j, i):
+            if not exists(j):
+                return
+            if i == 0:
+                result[j] = results.tile([P, ROW_TILES, C], F32, name="result")
+            for h in range(C // N_COLS):
+                classes = slice(h * N_COLS, (h + 1) * N_COLS)
+                if i * (C // N_COLS) + h < BANKS - SCALAR_BANKS:
+                    nc.vector.scalar_tensor_tensor(
+                        out=result[j][:, i, classes],
+                        in0=acc[j, i, h][:],
+                        scalar=INV_TEMPERATURE,
+                        in1=bias[:, classes],
+                        op0=ALU.mult,
+                        op1=ALU.add,
+                    )
+                else:
+                    nc.scalar.activation(
+                        out=result[j][:, i, classes],
+                        in_=acc[j, i, h][:],
+                        func=ACT.Copy,
+                        scale=INV_TEMPERATURE,
+                    )
+                    nc.gpsimd.tensor_tensor(
+                        out=result[j][:, i, classes],
+                        in0=result[j][:, i, classes],
+                        in1=bias[:, classes],
+                        op=ALU.add,
+                    )
+            nc.sync.dma_start(out=out_blocks[j][:, i, :], in_=result[j][:, i, :])
+
+        with tc.manual_schedule():
+            for j in range(-SHIFT_AHEAD, BLOCKS + 1):
+                turn(j + SHIFT_AHEAD)
+                finish(j - 1, 0)
+                quantise_block(j)
+                multiply(j, 0)
+                finish(j - 1, 1)
+                multiply(j, 1)
+                shift(j + SHIFT_AHEAD)
+                add_lr(j + ADD_AHEAD)

@@ -21,7 +21,9 @@ assert D == P * PACK
 ROW_TILES = 2
 BLOCK_ROWS = ROW_TILES * P
 BLOCKS = B * S // BLOCK_ROWS
-BLOCKS_PER_LOAD = 4
+BLOCKS_PER_LOAD = 2
+WC_LOADS = 2
+WC_TILES = C // P // WC_LOADS
 LOADS = BLOCKS // BLOCKS_PER_LOAD
 EXAMPLES = BLOCK_ROWS // S
 EXAMPLE_COLS = P // EXAMPLES
@@ -73,38 +75,30 @@ def tile_hetxlhead_pa_kernel(
         keep = ctx.enter_context(tc.tile_pool(name="keep", bufs=1))
         work = ctx.enter_context(tc.tile_pool(name="work", bufs=3))
         results = ctx.enter_context(tc.tile_pool(name="results", bufs=3))
-        turned = ctx.enter_context(tc.psum_pool(name="turned", bufs=4))
+        turned = ctx.enter_context(tc.psum_pool(name="turned", bufs=2))
         sums = ctx.enter_context(tc.psum_pool(name="sums", bufs=4))
+        ctx.enter_context(tc.manual_schedule())
 
-        def turn_weight(grouped, rows):
-            for g in range(rows.shape[1] // ROW_TILES):
-                pair = slice(g * ROW_TILES, (g + 1) * ROW_TILES)
-                bank = turned.tile([P, ROW_TILES, HALVES, P], F32, tag="turned")
-                turn_row_tiles(nc, bank[:], rows[:, pair], identity[:])
-                if g % 2 == 0:
-                    nc.vector.tensor_copy(
-                        out=grouped[:, pair].bitcast(F32), in_=halves_together(bank[:])
-                    )
-                else:
-                    nc.scalar.copy(out=grouped[:, pair].bitcast(F32), in_=halves_together(bank[:]))
+        bc_rows = keep.tile([P, C], BF16)
+        nc.vector.memset(bc_rows[:], 0.0)
 
-        identity = keep.tile([P, P], F32)
-        make_identity(nc, identity[:])
-        one = keep.tile([P, 1], F32)
-        nc.vector.memset(one[:], 1.0)
-        warm = keep.tile([P, 1], F32)
-        nc.scalar.activation(out=warm[:], in_=one[:], func=ACT.Exp)
-
+        bd_rows = keep.tile([P, PACK], BF16)
+        nc.scalar.dma_start(out=bd_rows[:], in_=b_diag.rearrange("(p t) -> p t", t=PACK))
         feat_rows = keep.tile([P, 1, D], BF16)
         nc.sync.dma_start(out=feat_rows[:, 0, :], in_=features)
         wd_rows = keep.tile([P, PACK, D], BF16)
         nc.sync.dma_start(out=wd_rows[:], in_=W_diag.rearrange("(r t) k -> r t k", t=PACK))
-        bd_rows = keep.tile([P, PACK], BF16)
-        nc.sync.dma_start(out=bd_rows[:], in_=b_diag.rearrange("(p t) -> p t", t=PACK))
+        wc_rows = []
+        for g in range(WC_LOADS):
+            wc_rows.append(keep.tile([P, WC_TILES, D], BF16, name="wc_rows%d" % g))
+            nc.sync.dma_start(
+                out=wc_rows[g][:],
+                in_=W_cls[g * WC_TILES * P : (g + 1) * WC_TILES * P].rearrange(
+                    "(i r) k -> r i k", r=P
+                ),
+            )
         noise_rows = []
         lr_rows = []
-        wc_rows = keep.tile([P, C // P, D], BF16)
-        bc_rows = keep.tile([P, C], BF16)
         for l in range(LOADS):
             noise_rows.append(
                 keep.tile([P, BLOCKS_PER_LOAD, ROW_TILES, D], BF16, name="noise_rows%d" % l)
@@ -115,64 +109,112 @@ def tile_hetxlhead_pa_kernel(
             )
             nc.sync.dma_start(out=lr_rows[l][:], in_=lr_loads[l])
             if l == 0:
-                nc.sync.dma_start(out=wc_rows[:], in_=W_cls.rearrange("(i r) k -> r i k", r=P))
-                nc.sync.dma_start(out=bc_rows[:], in_=b_cls.partition_broadcast(P))
+                nc.sync.dma_start(out=bc_rows[0:1, :], in_=b_cls.unsqueeze(0))
 
-        head_bank = turned.tile([P, ROW_TILES, HALVES, P], F32, tag="turned")
-        turn_row_tiles(nc, head_bank[:, 0:1], feat_rows[:], identity[:])
+        one = keep.tile([P, 1], F32)
+        nc.vector.memset(one[:], 1.0)
+        ones = keep.tile([P, P], BF16)
+        nc.vector.memset(ones[:], 1.0)
+        identity = keep.tile([P, P], F32)
+        make_identity(nc, identity[:])
+        warm = keep.tile([P, 1], F32)
+        nc.scalar.activation(out=warm[:], in_=one[:], func=ACT.Exp)
+
+        def turn_pair(rows):
+            bank = sums.tile([P, ROW_TILES, HALVES, P], F32, name="turned_pair", tag="sums")
+            turn_row_tiles(nc, bank[:, 0 : rows.shape[1]], rows, identity[:])
+            return bank
+
+        feat_bank = turn_pair(feat_rows[:])
+        wd_banks = [turn_pair(wd_rows[:, 2 * g : 2 * g + 2]) for g in range(2)]
         feat = keep.tile([P, 1, B, PACK], BF16, align_bytes=64)
-        nc.vector.tensor_copy(out=feat[:].bitcast(F32), in_=halves_together(head_bank[:, 0:1]))
-        feat32 = keep.tile([P, HALVES, B, PAIR], F32)
-        nc.vector.tensor_copy(
-            out=feat32[:].rearrange("p u b e -> p u (b e)"), in_=head_bank[:, 0].bitcast(BF16)
-        )
-        bd = keep.tile([P, PACK], F32)
-        nc.vector.tensor_copy(out=bd[:], in_=bd_rows[:])
-
-        wd = keep.tile([P, PACK, P, PACK], BF16, align_bytes=64)
-        turn_weight(wd, wd_rows)
+        nc.vector.tensor_copy(out=feat[:].bitcast(F32), in_=halves_together(feat_bank[:, 0:1]))
+        wd = [
+            keep.tile([P, ROW_TILES, P, PACK], BF16, name="wd%d" % g, align_bytes=64)
+            for g in range(2)
+        ]
+        nc.vector.tensor_copy(out=wd[0][:].bitcast(F32), in_=halves_together(wd_banks[0][:]))
+        nc.scalar.copy(out=wd[1][:].bitcast(F32), in_=halves_together(wd_banks[1][:]))
         feat_codes = keep.tile([P, B], U32, align_bytes=64)
         feat_scales = keep.tile([P, B], U8, align_bytes=64)
         quantise(nc, feat_codes[:], feat_scales[:], feat[:])
-        wd_codes = keep.tile([P, D], U32, align_bytes=64)
-        wd_scales = keep.tile([P, D], U8, align_bytes=64)
-        quantise(nc, wd_codes[:], wd_scales[:], wd[:])
+        bd = keep.tile([P, PACK], F32)
+        nc.vector.tensor_copy(out=bd[:], in_=bd_rows[:])
+        wd_codes = [keep.tile([P, ROW_TILES * P], U32, name="wd_codes%d" % g, align_bytes=64) for g in range(2)]
+        wd_scales = [keep.tile([P, ROW_TILES * P], U8, name="wd_scales%d" % g, align_bytes=64) for g in range(2)]
+        for g in range(2):
+            quantise(nc, wd_codes[g][:], wd_scales[g][:], wd[g][:])
 
-        z = sums.tile([P, PACK, B], F32, tag="sums")
+        z = sums.tile([P, PACK, B], F32, name="z", tag="sums")
         for t in range(PACK):
+            g, i = divmod(t, ROW_TILES)
             nc.tensor.matmul_mx(
                 out=z[:, t, :],
-                lhsT=wd_codes[:, t * P : (t + 1) * P].bitcast(FP8X4),
-                lhsT_scale=wd_scales[:, t * P : (t + 1) * P],
+                lhsT=wd_codes[g][:, i * P : (i + 1) * P].bitcast(FP8X4),
+                lhsT_scale=wd_scales[g][:, i * P : (i + 1) * P],
                 rhs=feat_codes[:].bitcast(FP8X4),
                 rhs_scale=feat_scales[:],
                 start=True,
                 stop=True,
             )
-        v = keep.tile([P, PACK, B], F32)
-        nc.vector.tensor_tensor(
-            out=v[:], in0=z[:], in1=bd[:].unsqueeze(2).to_broadcast([P, PACK, B]), op=ALU.add
-        )
         magnitude = keep.tile([P, PACK, B], F32)
-        nc.scalar.activation(out=magnitude[:], in_=v[:], func=ACT.Abs)
+        for t in range(PACK):
+            nc.scalar.activation(
+                out=magnitude[:, t], in_=z[:, t], func=ACT.Abs, bias=bd[:, t : t + 1]
+            )
         decay = keep.tile([P, PACK, B], F32)
         nc.scalar.activation(out=decay[:], in_=magnitude[:], func=ACT.Exp, scale=-1.0)
         log_term = keep.tile([P, PACK, B], F32)
         nc.scalar.activation(out=log_term[:], in_=decay[:], func=ACT.Ln, bias=one[:])
-        ramp = keep.tile([P, PACK, B], F32)
-        nc.vector.tensor_scalar(
-            out=ramp[:], in0=v[:], scalar1=0.0, scalar2=MIN_SCALE, op0=ALU.max, op1=ALU.add
-        )
-        std = keep.tile([P, PACK, B], F32)
-        nc.vector.tensor_tensor(out=std[:], in0=log_term[:], in1=ramp[:], op=ALU.add)
 
         wc = keep.tile([P, C // P, P, PACK], BF16, align_bytes=64)
-        turn_weight(wc, wc_rows)
+
+        def turn_classes(g):
+            l, i = divmod(g * ROW_TILES, WC_TILES)
+            bank = turn_pair(wc_rows[l][:, i : i + ROW_TILES])
+            nc.vector.tensor_copy(
+                out=wc[:, g * ROW_TILES : (g + 1) * ROW_TILES].bitcast(F32),
+                in_=halves_together(bank[:]),
+            )
+
+        turn_classes(0)
+        turn_classes(1)
+        turn_classes(2)
+        ramp = keep.tile([P, PACK, B], F32)
+        for t in range(PACK):
+            nc.vector.tensor_scalar(
+                out=ramp[:, t],
+                in0=z[:, t],
+                scalar1=bd[:, t : t + 1],
+                scalar2=0.0,
+                op0=ALU.add,
+                op1=ALU.max,
+            )
+        turn_classes(3)
+        feat32 = keep.tile([P, B, PACK], F32)
+        nc.vector.tensor_copy(out=feat32[:], in_=feat[:, 0])
+        std = keep.tile([P, PACK, B], F32)
+        nc.vector.scalar_tensor_tensor(
+            out=std[:],
+            in0=log_term[:],
+            scalar=MIN_SCALE,
+            in1=ramp[:],
+            op0=ALU.add,
+            op1=ALU.add,
+        )
         wc_codes = keep.tile([P, C], U32, align_bytes=64)
         wc_scales = keep.tile([P, C], U8, align_bytes=64)
         quantise(nc, wc_codes[:], wc_scales[:], wc[:])
+
         bias = keep.tile([P, C], F32)
-        nc.vector.tensor_scalar_mul(out=bias[:], in0=bc_rows[:], scalar1=INV_TEMPERATURE)
+
+        def spread_bias(h):
+            classes = slice(h * N_COLS, (h + 1) * N_COLS)
+            bank = sums.tile([P, N_COLS], F32, name="bias_bank", tag="sums")
+            nc.tensor.matmul(
+                bank[:], lhsT=ones[:], rhs=bc_rows[:, classes], start=True, stop=True
+            )
+            nc.vector.tensor_scalar_mul(out=bias[:, classes], in0=bank[:], scalar1=INV_TEMPERATURE)
 
         noise_bank, lr_bank, shifted = {}, {}, {}
         pre, pre_codes, pre_scales, acc, result = {}, {}, {}, {}, {}
@@ -185,10 +227,10 @@ def tile_hetxlhead_pa_kernel(
                 return
             l, k = divmod(j, BLOCKS_PER_LOAD)
             noise_bank[j] = turned.tile(
-                [P, ROW_TILES, HALVES, P], F32, name="noise_bank", tag="turned"
+                [P, ROW_TILES, HALVES, P], F32, name="noise_bank", tag="noise"
             )
             turn_row_tiles(nc, noise_bank[j][:], noise_rows[l][:, k], identity[:])
-            lr_bank[j] = turned.tile([P, ROW_TILES, HALVES, P], F32, name="lr_bank", tag="turned")
+            lr_bank[j] = turned.tile([P, ROW_TILES, HALVES, P], F32, name="lr_bank", tag="lr")
             turn_row_tiles(nc, lr_bank[j][:], lr_rows[l][:, k], identity[:])
 
         def shift(j):
@@ -210,7 +252,7 @@ def tile_hetxlhead_pa_kernel(
                         in_=noise_turned[:, :, u, cols, e],
                         func=ACT.Identity,
                         scale=std[:, t, b : b + 1],
-                        bias=feat32[:, u, b, e : e + 1],
+                        bias=feat32[:, b, t : t + 1],
                     )
 
         def add_lr(j):
@@ -279,13 +321,14 @@ def tile_hetxlhead_pa_kernel(
                     )
             nc.sync.dma_start(out=out_blocks[j][:, i, :], in_=result[j][:, i, :])
 
-        with tc.manual_schedule():
-            for j in range(-SHIFT_AHEAD, BLOCKS + 1):
-                turn(j + SHIFT_AHEAD)
-                finish(j - 1, 0)
-                quantise_block(j)
-                multiply(j, 0)
-                finish(j - 1, 1)
-                multiply(j, 1)
-                shift(j + SHIFT_AHEAD)
-                add_lr(j + ADD_AHEAD)
+        for j in range(-SHIFT_AHEAD, BLOCKS + 1):
+            turn(j + SHIFT_AHEAD)
+            finish(j - 1, 0)
+            quantise_block(j)
+            multiply(j, 0)
+            finish(j - 1, 1)
+            multiply(j, 1)
+            shift(j + SHIFT_AHEAD)
+            add_lr(j + ADD_AHEAD)
+            if j < 0:
+                spread_bias(j + SHIFT_AHEAD)

@@ -280,15 +280,16 @@ def tile_hetxlhead_pa_kernel(
             for h in range(C // N_COLS):
                 classes = slice(h * N_COLS, (h + 1) * N_COLS)
                 acc[j, i, h] = sums.tile([P, N_COLS], F32, name="acc", tag="sums")
-                nc.tensor.matmul_mx(
-                    out=acc[j, i, h][:],
-                    lhsT=pre_codes[j][:, i * P : (i + 1) * P].bitcast(FP8X4),
-                    lhsT_scale=pre_scales[j][:, i * P : (i + 1) * P],
-                    rhs=wc_codes[:, classes].bitcast(FP8X4),
-                    rhs_scale=wc_scales[:, classes],
-                    start=True,
-                    stop=True,
-                )
+                for repeat in range(2):
+                    nc.tensor.matmul_mx(
+                        out=acc[j, i, h][:],
+                        lhsT=pre_codes[j][:, i * P : (i + 1) * P].bitcast(FP8X4),
+                        lhsT_scale=pre_scales[j][:, i * P : (i + 1) * P],
+                        rhs=wc_codes[:, classes].bitcast(FP8X4),
+                        rhs_scale=wc_scales[:, classes],
+                        start=True,
+                        stop=True,
+                    )
 
         def finish(j, i):
             if not exists(j):

@@ -32,6 +32,8 @@ SHIFT_AHEAD = 2
 ADD_AHEAD = 1
 BANKS = ROW_TILES * (C // N_COLS)
 SCALAR_BANKS = 1
+LINE = 4
+LINES = P // LINE
 MIN_SCALE = 1e-3
 INV_TEMPERATURE = 1.0 / 1.5
 
@@ -42,7 +44,7 @@ def turn_row_tiles(nc, bank, rows, identity):
     for i in range(rows.shape[1]):
         words = rows[:, i, :].bitcast(F32)
         for u in range(HALVES):
-            nc.tensor.transpose(bank[:, i, u, :], words[:, u : HALVES * P : HALVES], identity)
+            nc.tensor.transpose(bank[:, i, u], words[:, u : HALVES * P : HALVES], identity)
 
 
 def halves_together(bank):
@@ -230,16 +232,20 @@ def tile_hetxlhead_pa_kernel(
                 [P, ROW_TILES, HALVES, P], F32, name="noise_bank", tag="noise"
             )
             turn_row_tiles(nc, noise_bank[j][:], noise_rows[l][:, k], identity[:])
-            lr_bank[j] = turned.tile([P, ROW_TILES, HALVES, P], F32, name="lr_bank", tag="lr")
-            turn_row_tiles(nc, lr_bank[j][:], lr_rows[l][:, k], identity[:])
+            lr_bank[j] = turned.tile(
+                [P, ROW_TILES, LINES, HALVES, LINE], F32, name="lr_bank", tag="lr"
+            )
+            turn_row_tiles(
+                nc, lr_bank[j][:].rearrange("p i c u n -> p i u c n"), lr_rows[l][:, k], identity[:]
+            )
 
         def shift(j):
             if not exists(j):
                 return
             noise_turned = work.tile([P, ROW_TILES, HALVES, P, PAIR], BF16)
             nc.scalar.copy(
-                out=noise_turned[:].rearrange("p i u r e -> p i u (r e)"),
-                in_=noise_bank[j][:].bitcast(BF16),
+                out=noise_turned[:].rearrange("p i u r e -> p i u (r e)").bitcast(F32),
+                in_=noise_bank[j][:],
             )
             shifted[j] = work.tile([P, ROW_TILES, PACK, P], F32, name="shifted")
             for m in range(EXAMPLES):
@@ -261,9 +267,9 @@ def tile_hetxlhead_pa_kernel(
             pre[j] = work.tile([P, ROW_TILES, P, PACK], BF16, name="pre", align_bytes=64)
             for i in range(ROW_TILES):
                 nc.vector.tensor_tensor(
-                    out=pre[j][:, i].rearrange("p r (u e) -> p r u e", e=PAIR),
-                    in0=lr_bank[j][:, i].bitcast(BF16).rearrange("p u (r e) -> p r u e", e=PAIR),
-                    in1=shifted[j][:, i].rearrange("p (u e) r -> p r u e", e=PAIR),
+                    out=pre[j][:, i].rearrange("p (c n) (u e) -> p c u e n", n=LINE, e=PAIR),
+                    in0=lr_bank[j][:, i].bitcast(BF16).rearrange("p c u (n e) -> p c u e n", e=PAIR),
+                    in1=shifted[j][:, i].rearrange("p (u e) (c n) -> p c u e n", n=LINE, e=PAIR),
                     op=ALU.add,
                 )
 
@@ -280,7 +286,7 @@ def tile_hetxlhead_pa_kernel(
             for h in range(C // N_COLS):
                 classes = slice(h * N_COLS, (h + 1) * N_COLS)
                 acc[j, i, h] = sums.tile([P, N_COLS], F32, name="acc", tag="sums")
-                for repeat in range(2):
+                for repeat in range(2 - h):
                     nc.tensor.matmul_mx(
                         out=acc[j, i, h][:],
                         lhsT=pre_codes[j][:, i * P : (i + 1) * P].bitcast(FP8X4),

@@ -22,6 +22,7 @@ ROW_TILES = 2
 BLOCK_ROWS = ROW_TILES * P
 BLOCKS = B * S // BLOCK_ROWS
 BLOCKS_PER_LOAD = 2
+WD_PAIRS = 2
 WC_LOADS = 2
 WC_TILES = C // P // WC_LOADS
 LOADS = BLOCKS // BLOCKS_PER_LOAD
@@ -30,8 +31,11 @@ EXAMPLE_COLS = P // EXAMPLES
 N_COLS = 512
 SHIFT_AHEAD = 2
 ADD_AHEAD = 1
-BANKS = ROW_TILES * (C // N_COLS)
-SCALAR_BANKS = 1
+SHIFTS = EXAMPLES * PACK
+GPSIMD_SHIFTS = 4
+GPSIMD_SHIFTS_FIRST = 3
+VECTOR_SHIFTS_FIRST = 8
+FIRST_EXAMPLES = SHIFT_AHEAD * EXAMPLES
 LINE = 4
 LINES = P // LINE
 MIN_SCALE = 1e-3
@@ -82,16 +86,22 @@ def tile_hetxlhead_pa_kernel(
         ctx.enter_context(tc.manual_schedule())
 
         bc_rows = keep.tile([P, C], BF16)
-        nc.vector.memset(bc_rows[:], 0.0)
+        nc.vector.memset(bc_rows[:].bitcast(F32), 0.0)
 
         bd_rows = keep.tile([P, PACK], BF16)
         nc.scalar.dma_start(out=bd_rows[:], in_=b_diag.rearrange("(p t) -> p t", t=PACK))
         feat_rows = keep.tile([P, 1, D], BF16)
         nc.sync.dma_start(out=feat_rows[:, 0, :], in_=features)
-        wd_rows = keep.tile([P, PACK, D], BF16)
-        nc.sync.dma_start(out=wd_rows[:], in_=W_diag.rearrange("(r t) k -> r t k", t=PACK))
-        wc_rows = []
-        for g in range(WC_LOADS):
+        wd_rows = []
+        for g in range(WD_PAIRS):
+            tiles = slice(g * ROW_TILES, (g + 1) * ROW_TILES)
+            wd_rows.append(keep.tile([P, ROW_TILES, D], BF16, name="wd_rows%d" % g))
+            nc.sync.dma_start(
+                out=wd_rows[g][:], in_=W_diag.rearrange("(r t) k -> r t k", t=PACK)[:, tiles]
+            )
+        wc_rows, noise_rows, lr_rows = [], [], []
+
+        def load_classes(g):
             wc_rows.append(keep.tile([P, WC_TILES, D], BF16, name="wc_rows%d" % g))
             nc.sync.dma_start(
                 out=wc_rows[g][:],
@@ -99,19 +109,21 @@ def tile_hetxlhead_pa_kernel(
                     "(i r) k -> r i k", r=P
                 ),
             )
-        noise_rows = []
-        lr_rows = []
-        for l in range(LOADS):
-            noise_rows.append(
-                keep.tile([P, BLOCKS_PER_LOAD, ROW_TILES, D], BF16, name="noise_rows%d" % l)
+
+        def load_samples(kind, rows, loads, l):
+            rows.append(
+                keep.tile([P, BLOCKS_PER_LOAD, ROW_TILES, D], BF16, name="%s_rows%d" % (kind, l))
             )
-            nc.sync.dma_start(out=noise_rows[l][:], in_=noise_loads[l])
-            lr_rows.append(
-                keep.tile([P, BLOCKS_PER_LOAD, ROW_TILES, D], BF16, name="lr_rows%d" % l)
-            )
-            nc.sync.dma_start(out=lr_rows[l][:], in_=lr_loads[l])
-            if l == 0:
-                nc.sync.dma_start(out=bc_rows[0:1, :], in_=b_cls.unsqueeze(0))
+            nc.sync.dma_start(out=rows[l][:], in_=loads[l])
+
+        load_classes(0)
+        load_samples("noise", noise_rows, noise_loads, 0)
+        load_classes(1)
+        load_samples("lr", lr_rows, lr_loads, 0)
+        nc.sync.dma_start(out=bc_rows[0:1, :], in_=b_cls.unsqueeze(0))
+        for l in range(1, LOADS):
+            load_samples("noise", noise_rows, noise_loads, l)
+            load_samples("lr", lr_rows, lr_loads, l)
 
         one = keep.tile([P, 1], F32)
         nc.vector.memset(one[:], 1.0)
@@ -128,7 +140,7 @@ def tile_hetxlhead_pa_kernel(
             return bank
 
         feat_bank = turn_pair(feat_rows[:])
-        wd_banks = [turn_pair(wd_rows[:, 2 * g : 2 * g + 2]) for g in range(2)]
+        wd_banks = [turn_pair(wd_rows[g][:]) for g in range(WD_PAIRS)]
         feat = keep.tile([P, 1, B, PACK], BF16, align_bytes=64)
         nc.vector.tensor_copy(out=feat[:].bitcast(F32), in_=halves_together(feat_bank[:, 0:1]))
         wd = [
@@ -137,11 +149,15 @@ def tile_hetxlhead_pa_kernel(
         ]
         nc.vector.tensor_copy(out=wd[0][:].bitcast(F32), in_=halves_together(wd_banks[0][:]))
         nc.scalar.copy(out=wd[1][:].bitcast(F32), in_=halves_together(wd_banks[1][:]))
+        feat32 = keep.tile([P, B, PACK], F32)
+        nc.scalar.copy(out=feat32[:], in_=feat[:, 0])
         feat_codes = keep.tile([P, B], U32, align_bytes=64)
         feat_scales = keep.tile([P, B], U8, align_bytes=64)
         quantise(nc, feat_codes[:], feat_scales[:], feat[:])
         bd = keep.tile([P, PACK], F32)
         nc.vector.tensor_copy(out=bd[:], in_=bd_rows[:])
+        bd_floor = keep.tile([P, PACK], F32)
+        nc.vector.tensor_scalar_add(out=bd_floor[:], in0=bd_rows[:], scalar1=MIN_SCALE)
         wd_codes = [keep.tile([P, ROW_TILES * P], U32, name="wd_codes%d" % g, align_bytes=64) for g in range(2)]
         wd_scales = [keep.tile([P, ROW_TILES * P], U8, name="wd_scales%d" % g, align_bytes=64) for g in range(2)]
         for g in range(2):
@@ -166,8 +182,10 @@ def tile_hetxlhead_pa_kernel(
             )
         decay = keep.tile([P, PACK, B], F32)
         nc.scalar.activation(out=decay[:], in_=magnitude[:], func=ACT.Exp, scale=-1.0)
-        log_term = keep.tile([P, PACK, B], F32)
-        nc.scalar.activation(out=log_term[:], in_=decay[:], func=ACT.Ln, bias=one[:])
+        parts = ((0, FIRST_EXAMPLES), (FIRST_EXAMPLES, B))
+        log_term = [keep.tile([P, PACK, hi - lo], F32, name="log_term%d" % lo) for lo, hi in parts]
+        std = [keep.tile([P, PACK, hi - lo], F32, name="std%d" % lo) for lo, hi in parts]
+
 
         wc = keep.tile([P, C // P, P, PACK], BF16, align_bytes=64)
 
@@ -179,52 +197,34 @@ def tile_hetxlhead_pa_kernel(
                 in_=halves_together(bank[:]),
             )
 
-        turn_classes(0)
-        turn_classes(1)
-        turn_classes(2)
-        ramp = keep.tile([P, PACK, B], F32)
-        for t in range(PACK):
-            nc.vector.tensor_scalar(
-                out=ramp[:, t],
-                in0=z[:, t],
-                scalar1=bd[:, t : t + 1],
-                scalar2=0.0,
-                op0=ALU.add,
-                op1=ALU.max,
+        def take_log(n):
+            lo, hi = parts[n]
+            nc.scalar.activation(
+                out=log_term[n][:], in_=decay[:, :, lo:hi], func=ACT.Ln, bias=one[:]
             )
-        turn_classes(3)
-        feat32 = keep.tile([P, B, PACK], F32)
-        nc.vector.tensor_copy(out=feat32[:], in_=feat[:, 0])
-        std = keep.tile([P, PACK, B], F32)
-        nc.vector.scalar_tensor_tensor(
-            out=std[:],
-            in0=log_term[:],
-            scalar=MIN_SCALE,
-            in1=ramp[:],
-            op0=ALU.add,
-            op1=ALU.add,
-        )
-        wc_codes = keep.tile([P, C], U32, align_bytes=64)
-        wc_scales = keep.tile([P, C], U8, align_bytes=64)
-        quantise(nc, wc_codes[:], wc_scales[:], wc[:])
 
-        bias = keep.tile([P, C], F32)
-
-        def spread_bias(h):
-            classes = slice(h * N_COLS, (h + 1) * N_COLS)
-            bank = sums.tile([P, N_COLS], F32, name="bias_bank", tag="sums")
-            nc.tensor.matmul(
-                bank[:], lhsT=ones[:], rhs=bc_rows[:, classes], start=True, stop=True
+        def make_std(n):
+            lo, hi = parts[n]
+            nc.vector.scalar_tensor_tensor(
+                out=std[n][:],
+                in0=v_floor[:, :, lo:hi],
+                scalar=MIN_SCALE,
+                in1=log_term[n][:],
+                op0=ALU.max,
+                op1=ALU.add,
             )
-            nc.vector.tensor_scalar_mul(out=bias[:, classes], in0=bank[:], scalar1=INV_TEMPERATURE)
 
-        noise_bank, lr_bank, shifted = {}, {}, {}
+        def std_column(t, b):
+            n = 0 if b < FIRST_EXAMPLES else 1
+            return std[n][:, t, b - parts[n][0] : b - parts[n][0] + 1]
+
+        noise_bank, noise_turned, lr_bank, shifted = {}, {}, {}, {}
         pre, pre_codes, pre_scales, acc, result = {}, {}, {}, {}, {}
 
         def exists(j):
             return 0 <= j < BLOCKS
 
-        def turn(j):
+        def turn_noise(j):
             if not exists(j):
                 return
             l, k = divmod(j, BLOCKS_PER_LOAD)
@@ -232,6 +232,11 @@ def tile_hetxlhead_pa_kernel(
                 [P, ROW_TILES, HALVES, P], F32, name="noise_bank", tag="noise"
             )
             turn_row_tiles(nc, noise_bank[j][:], noise_rows[l][:, k], identity[:])
+
+        def turn_lr(j):
+            if not exists(j):
+                return
+            l, k = divmod(j, BLOCKS_PER_LOAD)
             lr_bank[j] = turned.tile(
                 [P, ROW_TILES, LINES, HALVES, LINE], F32, name="lr_bank", tag="lr"
             )
@@ -239,26 +244,48 @@ def tile_hetxlhead_pa_kernel(
                 nc, lr_bank[j][:].rearrange("p i c u n -> p i u c n"), lr_rows[l][:, k], identity[:]
             )
 
+        def copy_noise(j):
+            if not exists(j):
+                return
+            noise_turned[j] = work.tile(
+                [P, ROW_TILES, HALVES, P, PAIR], BF16, name="noise_turned"
+            )
+            target = noise_turned[j][:].rearrange("p i u r e -> p i u (r e)").bitcast(F32)
+            if j == 0:
+                nc.vector.tensor_copy(out=target, in_=noise_bank[j][:])
+            else:
+                nc.scalar.copy(out=target, in_=noise_bank[j][:])
+
         def shift(j):
             if not exists(j):
                 return
-            noise_turned = work.tile([P, ROW_TILES, HALVES, P, PAIR], BF16)
-            nc.scalar.copy(
-                out=noise_turned[:].rearrange("p i u r e -> p i u (r e)").bitcast(F32),
-                in_=noise_bank[j][:],
-            )
             shifted[j] = work.tile([P, ROW_TILES, PACK, P], F32, name="shifted")
-            for m in range(EXAMPLES):
+            gpsimd_from = SHIFTS - (GPSIMD_SHIFTS_FIRST if j == 0 else GPSIMD_SHIFTS)
+            vector_from = gpsimd_from - (VECTOR_SHIFTS_FIRST if j == 0 else 0)
+            for n in range(SHIFTS):
+                m, t = divmod(n, PACK)
+                u, e = divmod(t, PAIR)
                 b = j * EXAMPLES + m
                 cols = slice(m * EXAMPLE_COLS, (m + 1) * EXAMPLE_COLS)
-                for t in range(PACK):
-                    u, e = divmod(t, PAIR)
+                target = shifted[j][:, :, t, cols]
+                noise = noise_turned[j][:, :, u, cols, e]
+                if n < vector_from:
                     nc.scalar.activation(
-                        out=shifted[j][:, :, t, cols],
-                        in_=noise_turned[:, :, u, cols, e],
+                        out=target,
+                        in_=noise,
                         func=ACT.Identity,
-                        scale=std[:, t, b : b + 1],
+                        scale=std_column(t, b),
                         bias=feat32[:, b, t : t + 1],
+                    )
+                else:
+                    engine = nc.vector if n < gpsimd_from else nc.gpsimd
+                    engine.tensor_scalar(
+                        out=target,
+                        in0=noise,
+                        scalar1=std_column(t, b),
+                        scalar2=feat32[:, b, t : t + 1],
+                        op0=ALU.mult,
+                        op1=ALU.add,
                     )
 
         def add_lr(j):
@@ -286,7 +313,7 @@ def tile_hetxlhead_pa_kernel(
             for h in range(C // N_COLS):
                 classes = slice(h * N_COLS, (h + 1) * N_COLS)
                 acc[j, i, h] = sums.tile([P, N_COLS], F32, name="acc", tag="sums")
-                for repeat in range(2 - h):
+                for repeat in range(2 if h == 0 and j < BLOCKS - 1 else 1):
                     nc.tensor.matmul_mx(
                         out=acc[j, i, h][:],
                         lhsT=pre_codes[j][:, i * P : (i + 1) * P].bitcast(FP8X4),
@@ -297,45 +324,124 @@ def tile_hetxlhead_pa_kernel(
                         stop=True,
                     )
 
-        def finish(j, i):
+        def result_half(j, i, h):
+            if j not in result:
+                result[j] = results.tile([P, ROW_TILES, C], F32, name="result")
+            return result[j][:, i, h * N_COLS : (h + 1) * N_COLS]
+
+        def scalar_banks(j):
+            if j == BLOCKS - 1:
+                return ()
+            if j == BLOCKS - 2:
+                return ((0, 1), (1, 1))
+            return ((1, 1),)
+
+        def finish(j, i, h):
             if not exists(j):
                 return
-            if i == 0:
-                result[j] = results.tile([P, ROW_TILES, C], F32, name="result")
-            for h in range(C // N_COLS):
-                classes = slice(h * N_COLS, (h + 1) * N_COLS)
-                if i * (C // N_COLS) + h < BANKS - SCALAR_BANKS:
-                    nc.vector.scalar_tensor_tensor(
-                        out=result[j][:, i, classes],
-                        in0=acc[j, i, h][:],
-                        scalar=INV_TEMPERATURE,
-                        in1=bias[:, classes],
-                        op0=ALU.mult,
-                        op1=ALU.add,
-                    )
-                else:
-                    nc.scalar.activation(
-                        out=result[j][:, i, classes],
-                        in_=acc[j, i, h][:],
-                        func=ACT.Copy,
-                        scale=INV_TEMPERATURE,
-                    )
-                    nc.gpsimd.tensor_tensor(
-                        out=result[j][:, i, classes],
-                        in0=result[j][:, i, classes],
-                        in1=bias[:, classes],
-                        op=ALU.add,
-                    )
-            nc.sync.dma_start(out=out_blocks[j][:, i, :], in_=result[j][:, i, :])
+            if (i, h) in scalar_banks(j):
+                finish_on_scalar(j, i, h)
+            else:
+                finish_on_vector(j, i, h)
 
-        for j in range(-SHIFT_AHEAD, BLOCKS + 1):
-            turn(j + SHIFT_AHEAD)
-            finish(j - 1, 0)
+        def finish_on_vector(j, i, h):
+            nc.vector.scalar_tensor_tensor(
+                out=result_half(j, i, h),
+                in0=acc[j, i, h][:],
+                scalar=INV_TEMPERATURE,
+                in1=bias[:, h * N_COLS : (h + 1) * N_COLS],
+                op0=ALU.mult,
+                op1=ALU.add,
+            )
+
+        def finish_on_scalar(j, i, h):
+            half = result_half(j, i, h)
+            nc.scalar.activation(
+                out=half, in_=acc[j, i, h][:], func=ACT.Copy, scale=INV_TEMPERATURE
+            )
+            nc.gpsimd.tensor_tensor(
+                out=half, in0=half, in1=bias[:, h * N_COLS : (h + 1) * N_COLS], op=ALU.add
+            )
+
+        def store(j, i):
+            if not exists(j):
+                return
+            pieces = 2 if (j, i) == (BLOCKS - 1, ROW_TILES - 1) else 1
+            for n in range(pieces):
+                classes = slice(n * C // pieces, (n + 1) * C // pieces)
+                nc.sync.dma_start(
+                    out=out_blocks[j][:, i, classes], in_=result[j][:, i, classes]
+                )
+
+        wc_codes = keep.tile([P, C], U32, align_bytes=64)
+        wc_scales = keep.tile([P, C], U8, align_bytes=64)
+
+        def quantise_classes(h):
+            tiles = C // P // 2
+            quantise(
+                nc,
+                wc_codes[:, h * N_COLS : (h + 1) * N_COLS],
+                wc_scales[:, h * N_COLS : (h + 1) * N_COLS],
+                wc[:, h * tiles : (h + 1) * tiles],
+            )
+
+        take_log(0)
+        turn_classes(0)
+        v_floor = keep.tile([P, PACK, B], F32)
+        nc.vector.tensor_tensor(
+            out=v_floor[:],
+            in0=z[:],
+            in1=bd_floor[:].unsqueeze(2).to_broadcast([P, PACK, B]),
+            op=ALU.add,
+        )
+        turn_noise(0)
+        turn_classes(1)
+        copy_noise(0)
+        make_std(0)
+        shift(0)
+        take_log(1)
+        turn_classes(2)
+        quantise_classes(0)
+        turn_noise(1)
+        turn_classes(3)
+        quantise_classes(1)
+        make_std(1)
+        turn_lr(0)
+        add_lr(0)
+        copy_noise(1)
+        shift(1)
+        turn_lr(1)
+        bias_banks = []
+        for h in range(C // N_COLS):
+            bias_banks.append(sums.tile([P, N_COLS], F32, name="bias_bank", tag="sums"))
+            nc.tensor.matmul(
+                bias_banks[h][:],
+                lhsT=ones[:],
+                rhs=bc_rows[:, h * N_COLS : (h + 1) * N_COLS],
+                start=True,
+                stop=True,
+            )
+        bias = keep.tile([P, C], F32)
+
+        for j in range(BLOCKS + 1):
+            turn_noise(j + SHIFT_AHEAD)
+            turn_lr(j + SHIFT_AHEAD)
+            finish(j - 1, 0, 0)
+            finish(j - 1, 0, 1)
+            store(j - 1, 0)
             quantise_block(j)
             multiply(j, 0)
-            finish(j - 1, 1)
+            if j == 0:
+                for h in range(C // N_COLS):
+                    nc.vector.tensor_scalar_mul(
+                        out=bias[:, h * N_COLS : (h + 1) * N_COLS],
+                        in0=bias_banks[h][:],
+                        scalar1=INV_TEMPERATURE,
+                    )
+            finish(j - 1, 1, 0)
+            finish(j - 1, 1, 1)
+            store(j - 1, 1)
             multiply(j, 1)
-            shift(j + SHIFT_AHEAD)
             add_lr(j + ADD_AHEAD)
-            if j < 0:
-                spread_bias(j + SHIFT_AHEAD)
+            copy_noise(j + SHIFT_AHEAD)
+            shift(j + SHIFT_AHEAD)

@@ -33,7 +33,6 @@ SHIFT_AHEAD = 2
 ADD_AHEAD = 1
 SHIFTS = EXAMPLES * PACK
 GPSIMD_SHIFTS = 4
-GPSIMD_SHIFTS_FIRST = 3
 VECTOR_SHIFTS_FIRST = 8
 FIRST_EXAMPLES = SHIFT_AHEAD * EXAMPLES
 LINE = 4
@@ -163,6 +162,18 @@ def tile_hetxlhead_pa_kernel(
         for g in range(2):
             quantise(nc, wd_codes[g][:], wd_scales[g][:], wd[g][:])
 
+        wc = keep.tile([P, C // P, P, PACK], BF16, align_bytes=64)
+
+        def turn_classes(g):
+            l, i = divmod(g * ROW_TILES, WC_TILES)
+            bank = turn_pair(wc_rows[l][:, i : i + ROW_TILES])
+            nc.vector.tensor_copy(
+                out=wc[:, g * ROW_TILES : (g + 1) * ROW_TILES].bitcast(F32),
+                in_=halves_together(bank[:]),
+            )
+
+        turn_classes(0)
+
         z = sums.tile([P, PACK, B], F32, name="z", tag="sums")
         for t in range(PACK):
             g, i = divmod(t, ROW_TILES)
@@ -185,17 +196,6 @@ def tile_hetxlhead_pa_kernel(
         parts = ((0, FIRST_EXAMPLES), (FIRST_EXAMPLES, B))
         log_term = [keep.tile([P, PACK, hi - lo], F32, name="log_term%d" % lo) for lo, hi in parts]
         std = [keep.tile([P, PACK, hi - lo], F32, name="std%d" % lo) for lo, hi in parts]
-
-
-        wc = keep.tile([P, C // P, P, PACK], BF16, align_bytes=64)
-
-        def turn_classes(g):
-            l, i = divmod(g * ROW_TILES, WC_TILES)
-            bank = turn_pair(wc_rows[l][:, i : i + ROW_TILES])
-            nc.vector.tensor_copy(
-                out=wc[:, g * ROW_TILES : (g + 1) * ROW_TILES].bitcast(F32),
-                in_=halves_together(bank[:]),
-            )
 
         def take_log(n):
             lo, hi = parts[n]
@@ -250,17 +250,16 @@ def tile_hetxlhead_pa_kernel(
             noise_turned[j] = work.tile(
                 [P, ROW_TILES, HALVES, P, PAIR], BF16, name="noise_turned"
             )
-            target = noise_turned[j][:].rearrange("p i u r e -> p i u (r e)").bitcast(F32)
-            if j == 0:
-                nc.vector.tensor_copy(out=target, in_=noise_bank[j][:])
-            else:
-                nc.scalar.copy(out=target, in_=noise_bank[j][:])
+            nc.scalar.copy(
+                out=noise_turned[j][:].rearrange("p i u r e -> p i u (r e)").bitcast(F32),
+                in_=noise_bank[j][:],
+            )
 
         def shift(j):
             if not exists(j):
                 return
             shifted[j] = work.tile([P, ROW_TILES, PACK, P], F32, name="shifted")
-            gpsimd_from = SHIFTS - (GPSIMD_SHIFTS_FIRST if j == 0 else GPSIMD_SHIFTS)
+            gpsimd_from = SHIFTS - GPSIMD_SHIFTS
             vector_from = gpsimd_from - (VECTOR_SHIFTS_FIRST if j == 0 else 0)
             for n in range(SHIFTS):
                 m, t = divmod(n, PACK)
@@ -306,6 +305,8 @@ def tile_hetxlhead_pa_kernel(
             pre_codes[j] = work.tile([P, BLOCK_ROWS], U32, name="pre_codes", align_bytes=64)
             pre_scales[j] = work.tile([P, BLOCK_ROWS], U8, name="pre_scales", align_bytes=64)
             quantise(nc, pre_codes[j][:], pre_scales[j][:], pre[j][:])
+            behind = work.tile([P, 1], U32, name="behind")
+            nc.gpsimd.tensor_copy(out=behind[:], in_=pre_codes[j][:, 0:1])
 
         def multiply(j, i):
             if not exists(j):
@@ -386,7 +387,6 @@ def tile_hetxlhead_pa_kernel(
             )
 
         take_log(0)
-        turn_classes(0)
         v_floor = keep.tile([P, PACK, B], F32)
         nc.vector.tensor_tensor(
             out=v_floor[:],
@@ -396,16 +396,15 @@ def tile_hetxlhead_pa_kernel(
         )
         turn_noise(0)
         turn_classes(1)
-        copy_noise(0)
-        make_std(0)
-        shift(0)
-        take_log(1)
         turn_classes(2)
         quantise_classes(0)
+        make_std(0)
+        copy_noise(0)
         turn_noise(1)
         turn_classes(3)
         quantise_classes(1)
-        make_std(1)
+        shift(0)
+        take_log(1)
         turn_lr(0)
         add_lr(0)
         copy_noise(1)
@@ -432,6 +431,7 @@ def tile_hetxlhead_pa_kernel(
             quantise_block(j)
             multiply(j, 0)
             if j == 0:
+                make_std(1)
                 for h in range(C // N_COLS):
                     nc.vector.tensor_scalar_mul(
                         out=bias[:, h * N_COLS : (h + 1) * N_COLS],

from contextlib import ExitStack

import concourse.mybir as mybir
from concourse.masks import make_identity

F32 = mybir.dt.float32
BF16 = mybir.dt.bfloat16
U32 = mybir.dt.uint32
U8 = mybir.dt.uint8
FP8X4 = mybir.dt.float8_e4m3fn_x4
ACT = mybir.ActivationFunctionType
ALU = mybir.AluOpType

P = 128
PAIR = 2
HALVES = 2
PACK = HALVES * PAIR
B, S, D, C = 128, 32, 512, 1024
assert D == P * PACK

ROW_TILES = 2
BLOCK_ROWS = ROW_TILES * P
BLOCKS = B * S // BLOCK_ROWS
BLOCKS_PER_LOAD = 2
WD_PAIRS = 2
WC_LOADS = 2
WC_TILES = C // P // WC_LOADS
LOADS = BLOCKS // BLOCKS_PER_LOAD
EXAMPLES = BLOCK_ROWS // S
EXAMPLE_COLS = P // EXAMPLES
N_COLS = 512
SHIFT_AHEAD = 2
ADD_AHEAD = 1
SHIFTS = EXAMPLES * PACK
GPSIMD_SHIFTS = 4
VECTOR_SHIFTS_FIRST = 8
FIRST_EXAMPLES = SHIFT_AHEAD * EXAMPLES
LINE = 4
LINES = P // LINE
MIN_SCALE = 1e-3
INV_TEMPERATURE = 1.0 / 1.5

FLOPS = 2 * B * S * D * C + 2 * B * D * D


def turn_row_tiles(nc, bank, rows, identity):
    for i in range(rows.shape[1]):
        words = rows[:, i, :].bitcast(F32)
        for u in range(HALVES):
            nc.tensor.transpose(bank[:, i, u], words[:, u : HALVES * P : HALVES], identity)


def halves_together(bank):
    return bank.rearrange("p i u r -> p i r u")


def quantise(nc, codes, scales, grouped):
    nc.vector.quantize_mx(
        out=codes.bitcast(FP8X4),
        scales=scales,
        in_=grouped.rearrange("p i r t -> p (i r t)"),
    )


def tile_hetxlhead_pa_kernel(
    tc, features, W_diag, b_diag, W_cls, b_cls, noise_diag, lr_samples, out
):
    nc = tc.nc
    noise_loads = noise_diag.rearrange("b s d -> (b s) d").rearrange(
        "(l j p i) d -> l p j i d", j=BLOCKS_PER_LOAD, p=P, i=ROW_TILES
    )
    lr_loads = lr_samples.rearrange("b s d -> (b s) d").rearrange(
        "(l j p i) d -> l p j i d", j=BLOCKS_PER_LOAD, p=P, i=ROW_TILES
    )
    out_blocks = out.rearrange("b s c -> (b s) c").rearrange(
        "(j p i) c -> j p i c", p=P, i=ROW_TILES
    )

    with ExitStack() as ctx:
        keep = ctx.enter_context(tc.tile_pool(name="keep", bufs=1))
        work = ctx.enter_context(tc.tile_pool(name="work", bufs=3))
        results = ctx.enter_context(tc.tile_pool(name="results", bufs=3))
        turned = ctx.enter_context(tc.psum_pool(name="turned", bufs=2))
        sums = ctx.enter_context(tc.psum_pool(name="sums", bufs=4))
        ctx.enter_context(tc.manual_schedule())

        bc_rows = keep.tile([P, C], BF16)
        nc.vector.memset(bc_rows[:].bitcast(F32), 0.0)

        bd_rows = keep.tile([P, PACK], BF16)
        nc.scalar.dma_start(out=bd_rows[:], in_=b_diag.rearrange("(p t) -> p t", t=PACK))
        feat_rows = keep.tile([P, 1, D], BF16)
        nc.sync.dma_start(out=feat_rows[:, 0, :], in_=features)
        wd_rows = []
        for g in range(WD_PAIRS):
            tiles = slice(g * ROW_TILES, (g + 1) * ROW_TILES)
            wd_rows.append(keep.tile([P, ROW_TILES, D], BF16, name="wd_rows%d" % g))
            nc.sync.dma_start(
                out=wd_rows[g][:], in_=W_diag.rearrange("(r t) k -> r t k", t=PACK)[:, tiles]
            )
        wc_rows, noise_rows, lr_rows = [], [], []

        def load_classes(g):
            wc_rows.append(keep.tile([P, WC_TILES, D], BF16, name="wc_rows%d" % g))
            nc.sync.dma_start(
                out=wc_rows[g][:],
                in_=W_cls[g * WC_TILES * P : (g + 1) * WC_TILES * P].rearrange(
                    "(i r) k -> r i k", r=P
                ),
            )

        def load_samples(kind, rows, loads, l):
            rows.append(
                keep.tile([P, BLOCKS_PER_LOAD, ROW_TILES, D], BF16, name="%s_rows%d" % (kind, l))
            )
            nc.sync.dma_start(out=rows[l][:], in_=loads[l])

        load_classes(0)
        load_samples("noise", noise_rows, noise_loads, 0)
        load_classes(1)
        load_samples("lr", lr_rows, lr_loads, 0)
        nc.sync.dma_start(out=bc_rows[0:1, :], in_=b_cls.unsqueeze(0))
        for l in range(1, LOADS):
            load_samples("noise", noise_rows, noise_loads, l)
            load_samples("lr", lr_rows, lr_loads, l)

        one = keep.tile([P, 1], F32)
        nc.vector.memset(one[:], 1.0)
        ones = keep.tile([P, P], BF16)
        nc.vector.memset(ones[:], 1.0)
        identity = keep.tile([P, P], F32)
        make_identity(nc, identity[:])
        warm = keep.tile([P, 1], F32)
        nc.scalar.activation(out=warm[:], in_=one[:], func=ACT.Exp)

        def turn_pair(rows):
            bank = sums.tile([P, ROW_TILES, HALVES, P], F32, name="turned_pair", tag="sums")
            turn_row_tiles(nc, bank[:, 0 : rows.shape[1]], rows, identity[:])
            return bank

        feat_bank = turn_pair(feat_rows[:])
        wd_banks = [turn_pair(wd_rows[g][:]) for g in range(WD_PAIRS)]
        feat = keep.tile([P, 1, B, PACK], BF16, align_bytes=64)
        nc.vector.tensor_copy(out=feat[:].bitcast(F32), in_=halves_together(feat_bank[:, 0:1]))
        wd = [
            keep.tile([P, ROW_TILES, P, PACK], BF16, name="wd%d" % g, align_bytes=64)
            for g in range(2)
        ]
        nc.vector.tensor_copy(out=wd[0][:].bitcast(F32), in_=halves_together(wd_banks[0][:]))
        nc.scalar.copy(out=wd[1][:].bitcast(F32), in_=halves_together(wd_banks[1][:]))
        feat32 = keep.tile([P, B, PACK], F32)
        nc.scalar.copy(out=feat32[:], in_=feat[:, 0])
        feat_codes = keep.tile([P, B], U32, align_bytes=64)
        feat_scales = keep.tile([P, B], U8, align_bytes=64)
        quantise(nc, feat_codes[:], feat_scales[:], feat[:])
        bd = keep.tile([P, PACK], F32)
        nc.vector.tensor_copy(out=bd[:], in_=bd_rows[:])
        bd_floor = keep.tile([P, PACK], F32)
        nc.vector.tensor_scalar_add(out=bd_floor[:], in0=bd_rows[:], scalar1=MIN_SCALE)
        wd_codes = [keep.tile([P, ROW_TILES * P], U32, name="wd_codes%d" % g, align_bytes=64) for g in range(2)]
        wd_scales = [keep.tile([P, ROW_TILES * P], U8, name="wd_scales%d" % g, align_bytes=64) for g in range(2)]
        for g in range(2):
            quantise(nc, wd_codes[g][:], wd_scales[g][:], wd[g][:])

        wc = keep.tile([P, C // P, P, PACK], BF16, align_bytes=64)

        def turn_classes(g):
            l, i = divmod(g * ROW_TILES, WC_TILES)
            bank = turn_pair(wc_rows[l][:, i : i + ROW_TILES])
            nc.vector.tensor_copy(
                out=wc[:, g * ROW_TILES : (g + 1) * ROW_TILES].bitcast(F32),
                in_=halves_together(bank[:]),
            )

        turn_classes(0)

        z = sums.tile([P, PACK, B], F32, name="z", tag="sums")
        for t in range(PACK):
            g, i = divmod(t, ROW_TILES)
            nc.tensor.matmul_mx(
                out=z[:, t, :],
                lhsT=wd_codes[g][:, i * P : (i + 1) * P].bitcast(FP8X4),
                lhsT_scale=wd_scales[g][:, i * P : (i + 1) * P],
                rhs=feat_codes[:].bitcast(FP8X4),
                rhs_scale=feat_scales[:],
                start=True,
                stop=True,
            )
        magnitude = keep.tile([P, PACK, B], F32)
        for t in range(PACK):
            nc.scalar.activation(
                out=magnitude[:, t], in_=z[:, t], func=ACT.Abs, bias=bd[:, t : t + 1]
            )
        decay = keep.tile([P, PACK, B], F32)
        nc.scalar.activation(out=decay[:], in_=magnitude[:], func=ACT.Exp, scale=-1.0)
        parts = ((0, FIRST_EXAMPLES), (FIRST_EXAMPLES, B))
        log_term = [keep.tile([P, PACK, hi - lo], F32, name="log_term%d" % lo) for lo, hi in parts]
        std = [keep.tile([P, PACK, hi - lo], F32, name="std%d" % lo) for lo, hi in parts]

        def take_log(n):
            lo, hi = parts[n]
            nc.scalar.activation(
                out=log_term[n][:], in_=decay[:, :, lo:hi], func=ACT.Ln, bias=one[:]
            )

        def make_std(n):
            lo, hi = parts[n]
            nc.vector.scalar_tensor_tensor(
                out=std[n][:],
                in0=v_floor[:, :, lo:hi],
                scalar=MIN_SCALE,
                in1=log_term[n][:],
                op0=ALU.max,
                op1=ALU.add,
            )

        def std_column(t, b):
            n = 0 if b < FIRST_EXAMPLES else 1
            return std[n][:, t, b - parts[n][0] : b - parts[n][0] + 1]

        noise_bank, noise_turned, lr_bank, shifted = {}, {}, {}, {}
        pre, pre_codes, pre_scales, acc, result = {}, {}, {}, {}, {}

        def exists(j):
            return 0 <= j < BLOCKS

        def turn_noise(j):
            if not exists(j):
                return
            l, k = divmod(j, BLOCKS_PER_LOAD)
            noise_bank[j] = turned.tile(
                [P, ROW_TILES, HALVES, P], F32, name="noise_bank", tag="noise"
            )
            turn_row_tiles(nc, noise_bank[j][:], noise_rows[l][:, k], identity[:])

        def turn_lr(j):
            if not exists(j):
                return
            l, k = divmod(j, BLOCKS_PER_LOAD)
            lr_bank[j] = turned.tile(
                [P, ROW_TILES, LINES, HALVES, LINE], F32, name="lr_bank", tag="lr"
            )
            turn_row_tiles(
                nc, lr_bank[j][:].rearrange("p i c u n -> p i u c n"), lr_rows[l][:, k], identity[:]
            )

        def copy_noise(j):
            if not exists(j):
                return
            noise_turned[j] = work.tile(
                [P, ROW_TILES, HALVES, P, PAIR], BF16, name="noise_turned"
            )
            nc.scalar.copy(
                out=noise_turned[j][:].rearrange("p i u r e -> p i u (r e)").bitcast(F32),
                in_=noise_bank[j][:],
            )

        def shift(j):
            if not exists(j):
                return
            shifted[j] = work.tile([P, ROW_TILES, PACK, P], F32, name="shifted")
            gpsimd_from = SHIFTS - GPSIMD_SHIFTS
            vector_from = gpsimd_from - (VECTOR_SHIFTS_FIRST if j == 0 else 0)
            for n in range(SHIFTS):
                m, t = divmod(n, PACK)
                u, e = divmod(t, PAIR)
                b = j * EXAMPLES + m
                cols = slice(m * EXAMPLE_COLS, (m + 1) * EXAMPLE_COLS)
                target = shifted[j][:, :, t, cols]
                noise = noise_turned[j][:, :, u, cols, e]
                if n < vector_from:
                    nc.scalar.activation(
                        out=target,
                        in_=noise,
                        func=ACT.Identity,
                        scale=std_column(t, b),
                        bias=feat32[:, b, t : t + 1],
                    )
                else:
                    engine = nc.vector if n < gpsimd_from else nc.gpsimd
                    engine.tensor_scalar(
                        out=target,
                        in0=noise,
                        scalar1=std_column(t, b),
                        scalar2=feat32[:, b, t : t + 1],
                        op0=ALU.mult,
                        op1=ALU.add,
                    )

        def add_lr(j):
            if not exists(j):
                return
            pre[j] = work.tile([P, ROW_TILES, P, PACK], BF16, name="pre", align_bytes=64)
            for i in range(ROW_TILES):
                nc.vector.tensor_tensor(
                    out=pre[j][:, i].rearrange("p (c n) (u e) -> p c u e n", n=LINE, e=PAIR),
                    in0=lr_bank[j][:, i].bitcast(BF16).rearrange("p c u (n e) -> p c u e n", e=PAIR),
                    in1=shifted[j][:, i].rearrange("p (u e) (c n) -> p c u e n", n=LINE, e=PAIR),
                    op=ALU.add,
                )

        def quantise_block(j):
            if not exists(j):
                return
            pre_codes[j] = work.tile([P, BLOCK_ROWS], U32, name="pre_codes", align_bytes=64)
            pre_scales[j] = work.tile([P, BLOCK_ROWS], U8, name="pre_scales", align_bytes=64)
            quantise(nc, pre_codes[j][:], pre_scales[j][:], pre[j][:])
            behind = work.tile([P, 1], U32, name="behind")
            nc.gpsimd.tensor_copy(out=behind[:], in_=pre_codes[j][:, 0:1])

        def multiply(j, i):
            if not exists(j):
                return
            for h in range(C // N_COLS):
                classes = slice(h * N_COLS, (h + 1) * N_COLS)
                acc[j, i, h] = sums.tile([P, N_COLS], F32, name="acc", tag="sums")
                for repeat in range(2 if h == 0 and j < BLOCKS - 1 else 1):
                    nc.tensor.matmul_mx(
                        out=acc[j, i, h][:],
                        lhsT=pre_codes[j][:, i * P : (i + 1) * P].bitcast(FP8X4),
                        lhsT_scale=pre_scales[j][:, i * P : (i + 1) * P],
                        rhs=wc_codes[:, classes].bitcast(FP8X4),
                        rhs_scale=wc_scales[:, classes],
                        start=True,
                        stop=True,
                    )

        def result_half(j, i, h):
            if j not in result:
                result[j] = results.tile([P, ROW_TILES, C], F32, name="result")
            return result[j][:, i, h * N_COLS : (h + 1) * N_COLS]

        def scalar_banks(j):
            if j == BLOCKS - 1:
                return ()
            if j == BLOCKS - 2:
                return ((0, 1), (1, 1))
            return ((1, 1),)

        def finish(j, i, h):
            if not exists(j):
                return
            if (i, h) in scalar_banks(j):
                finish_on_scalar(j, i, h)
            else:
                finish_on_vector(j, i, h)

        def finish_on_vector(j, i, h):
            nc.vector.scalar_tensor_tensor(
                out=result_half(j, i, h),
                in0=acc[j, i, h][:],
                scalar=INV_TEMPERATURE,
                in1=bias[:, h * N_COLS : (h + 1) * N_COLS],
                op0=ALU.mult,
                op1=ALU.add,
            )

        def finish_on_scalar(j, i, h):
            half = result_half(j, i, h)
            nc.scalar.activation(
                out=half, in_=acc[j, i, h][:], func=ACT.Copy, scale=INV_TEMPERATURE
            )
            nc.gpsimd.tensor_tensor(
                out=half, in0=half, in1=bias[:, h * N_COLS : (h + 1) * N_COLS], op=ALU.add
            )

        def store(j, i):
            if not exists(j):
                return
            pieces = 2 if (j, i) == (BLOCKS - 1, ROW_TILES - 1) else 1
            for n in range(pieces):
                classes = slice(n * C // pieces, (n + 1) * C // pieces)
                nc.sync.dma_start(
                    out=out_blocks[j][:, i, classes], in_=result[j][:, i, classes]
                )

        wc_codes = keep.tile([P, C], U32, align_bytes=64)
        wc_scales = keep.tile([P, C], U8, align_bytes=64)

        def quantise_classes(h):
            tiles = C // P // 2
            quantise(
                nc,
                wc_codes[:, h * N_COLS : (h + 1) * N_COLS],
                wc_scales[:, h * N_COLS : (h + 1) * N_COLS],
                wc[:, h * tiles : (h + 1) * tiles],
            )

        take_log(0)
        v_floor = keep.tile([P, PACK, B], F32)
        nc.vector.tensor_tensor(
            out=v_floor[:],
            in0=z[:],
            in1=bd_floor[:].unsqueeze(2).to_broadcast([P, PACK, B]),
            op=ALU.add,
        )
        turn_noise(0)
        turn_classes(1)
        turn_classes(2)
        quantise_classes(0)
        make_std(0)
        copy_noise(0)
        turn_noise(1)
        turn_classes(3)
        quantise_classes(1)
        shift(0)
        take_log(1)
        turn_lr(0)
        add_lr(0)
        copy_noise(1)
        shift(1)
        turn_lr(1)
        bias_banks = []
        for h in range(C // N_COLS):
            bias_banks.append(sums.tile([P, N_COLS], F32, name="bias_bank", tag="sums"))
            nc.tensor.matmul(
                bias_banks[h][:],
                lhsT=ones[:],
                rhs=bc_rows[:, h * N_COLS : (h + 1) * N_COLS],
                start=True,
                stop=True,
            )
        bias = keep.tile([P, C], F32)

        for j in range(BLOCKS + 1):
            turn_noise(j + SHIFT_AHEAD)
            turn_lr(j + SHIFT_AHEAD)
            finish(j - 1, 0, 0)
            finish(j - 1, 0, 1)
            store(j - 1, 0)
            quantise_block(j)
            multiply(j, 0)
            if j == 0:
                make_std(1)
                for h in range(C // N_COLS):
                    nc.vector.tensor_scalar_mul(
                        out=bias[:, h * N_COLS : (h + 1) * N_COLS],
                        in0=bias_banks[h][:],
                        scalar1=INV_TEMPERATURE,
                    )
            finish(j - 1, 1, 0)
            finish(j - 1, 1, 1)
            store(j - 1, 1)
            multiply(j, 1)
            add_lr(j + ADD_AHEAD)
            copy_noise(j + SHIFT_AHEAD)
            shift(j + SHIFT_AHEAD)
